import numpy as np
import ml_dtypes


def mxq(x, axis, fmt="e4m3"):
    dtype, down = {"e4m3": (ml_dtypes.float8_e4m3fn, 7), "e5m2": (ml_dtypes.float8_e5m2, 14)}[fmt]
    v = np.moveaxis(np.asarray(x, np.float32).astype(ml_dtypes.bfloat16).astype(np.float64), axis, -1)
    blocks = v.reshape(v.shape[:-1] + (-1, 32))
    amax = np.abs(blocks).max(-1, keepdims=True)
    byte = np.maximum(np.where(amax > 0, np.frexp(amax)[1] - 1 + 127, 0) - down, 1)
    scale = np.exp2(byte - 127.0)
    codes = (blocks / scale).astype(np.float32).astype(dtype).astype(np.float64)
    return np.moveaxis((codes * scale).reshape(v.shape), -1, axis)


WIDE = False


def mx_kscale(k):
    if not WIDE:
        return np.ones(k)
    levels = np.array([10, -10, 5, -5, 0])
    a = np.random.permutation(np.resize(levels, k // 512 * 4)).reshape(k // 512, 4)
    idx = np.arange(k)
    return np.exp2(a[idx // 512, idx % 128 // 32])


BF16 = ml_dtypes.bfloat16


def bf(x):
    return np.asarray(x, np.float32).astype(BF16)


def f64(x):
    return np.asarray(x).astype(np.float64)


B, C, K, BK, BN = 1024, 2048, 2048, 1, 16
KEEP = 0.3


def setup_inputs():
    s = mx_kscale(C)
    x = np.random.standard_normal((B, C)) * s
    weight = np.random.uniform(-1.0, 1.0, (K, C)) * 3.2 / np.sqrt(C)
    blk = (np.random.uniform(0.0, 1.0, (K // BK, C // BN)) < KEEP).astype(np.float64)
    mask = np.repeat(np.repeat(blk, BK, axis=0), BN, axis=1)
    weight = weight * mask / s[None, :]
    bias = np.random.uniform(-1.0, 1.0, K) * 0.5
    return {"x": bf(x), "weight": bf(weight), "bias": bf(bias)}


def reference(x, weight, bias):
    return np.maximum((mxq(f64(x), 1, "e4m3") @ mxq(f64(weight), 1, "e4m3").T) + f64(bias), 0.0)

@@ -1,0 +1,185 @@
+from contextlib import ExitStack
+
+import concourse.mybir as mybir
+from concourse.masks import make_identity
+
+F32 = mybir.dt.float32
+BF16 = mybir.dt.bfloat16
+U32 = mybir.dt.uint32
+U8 = mybir.dt.uint8
+FP8X4 = mybir.dt.float8_e4m3fn_x4
+ADD = mybir.AluOpType.add
+RELU = mybir.ActivationFunctionType.Relu
+
+P = 128
+B, C, K = 1024, 2048, 2048
+FLOPS = 2 * B * C * K
+PINNED = True
+
+M_TILES = B // P
+CHUNK = 512
+N_CHUNKS = K // CHUNK
+PASSES = C // 512
+
+
+def tile_sparselinearrelu_kernel(tc, x, weight, bias, out):
+    nc = tc.nc
+    with ExitStack() as ctx:
+        if PINNED:
+            ctx.enter_context(tc.manual_schedule())
+        keep = ctx.enter_context(tc.tile_pool(name="keep", bufs=1))
+        grp_pool = ctx.enter_context(tc.tile_pool(name="grp", bufs=8))
+        st_pool = ctx.enter_context(tc.tile_pool(name="st", bufs=8))
+        tp_pool = ctx.enter_context(tc.psum_pool(name="tp", bufs=4))
+        acc_pool = ctx.enter_context(tc.psum_pool(name="acc", bufs=4))
+
+        x_view = x.rearrange("(p t) k -> p t k", t=M_TILES)
+        out_view = out.rearrange("(p t) n -> t p n", t=M_TILES)
+        w_view = weight.rearrange("(j p) k -> p j k", p=P)
+
+        ident = keep.tile([P, P], F32, name="ident")
+        make_identity(nc, ident[:])
+        brow = keep.tile([P, K], BF16, name="brow")
+        nc.vector.memset(brow[:], 0.0)
+        nc.sync.dma_start(out=brow[0:1, :], in_=bias.rearrange("(o n) -> o n", o=1))
+        ones = keep.tile([P, P], BF16, name="ones")
+        nc.vector.memset(ones[:], 1.0)
+
+        w_sb = {}
+        x_sb = {}
+
+        def load_w(c, h):
+            t = keep.tile([P, 2, C], BF16, name="w_sb_%d_%d" % (c, h))
+            j0 = 4 * c + 2 * h
+            nc.sync.dma_start(out=t[:], in_=w_view[:, j0:j0 + 2, :])
+            w_sb[(c, h)] = t
+
+        def load_x(i):
+            t = keep.tile([P, 2, C], BF16, name="x_sb_%d" % i)
+            nc.sync.dma_start(out=t[:], in_=x_view[:, 2 * i:2 * i + 2, :])
+            x_sb[i] = t
+
+        load_w(0, 0)
+        load_w(0, 1)
+        for i in range(4):
+            load_x(i)
+        for c in range(1, N_CHUNKS):
+            load_w(c, 0)
+            load_w(c, 1)
+
+        xq = [keep.tile([P, PASSES * P], U32, name="xq_%d" % m, align_bytes=64) for m in range(M_TILES)]
+        xs = [keep.tile([P, PASSES * P], U8, name="xs_%d" % m, align_bytes=64) for m in range(M_TILES)]
+        wq = [[keep.tile([P, CHUNK], U32, name="wq_%d_%d" % (c, g), align_bytes=64) for g in range(PASSES)]
+              for c in range(N_CHUNKS)]
+        ws = [[keep.tile([P, CHUNK], U8, name="ws_%d_%d" % (c, g), align_bytes=64) for g in range(PASSES)]
+              for c in range(N_CHUNKS)]
+
+        bias_bc = keep.tile([P, K], F32, name="bias_bc")
+        for c in range(N_CHUNKS):
+            cols = slice(c * CHUNK, (c + 1) * CHUNK)
+            bacc = acc_pool.tile([P, CHUNK], F32, name="acc")
+            nc.tensor.matmul(out=bacc[:], lhsT=ones[:], rhs=brow[:, cols], start=True, stop=True)
+            if c % 2 == 0:
+                nc.vector.tensor_copy(out=bias_bc[:, cols], in_=bacc[:])
+            else:
+                nc.scalar.copy(out=bias_bc[:, cols], in_=bacc[:])
+
+        def w_unit(c, h, g):
+            srcs = [w_sb[(c, h)][:, j, :].bitcast(F32)[:, 256 * g:256 * g + 256] for j in range(2)]
+            cols = slice(256 * h, 256 * h + 256)
+            return srcs, wq[c][g][:, cols], ws[c][g][:, cols]
+
+        def x_unit(m, gp):
+            row = x_sb[m // 2][:, m % 2, :].bitcast(F32)
+            srcs = [row[:, 256 * (2 * gp + a):256 * (2 * gp + a) + 256] for a in range(2)]
+            cols = slice(256 * gp, 256 * gp + 256)
+            return srcs, xq[m][:, cols], xs[m][:, cols]
+
+        def transposes(unit):
+            bank = tp_pool.tile([P, 2, 2, P], F32, name="bank")
+            for a in range(2):
+                for u in range(2):
+                    nc.tensor.transpose(bank[:, a, u, :], unit[0][a][:, P * u:P * u + P], ident[:])
+            return bank
+
+        def leave(engine_copy, bank):
+            grouped = grp_pool.tile([P, 1024], BF16, name="grouped", align_bytes=64)
+            engine_copy(
+                out=grouped[:].bitcast(F32).rearrange("p (a c u) -> p a c u", a=2, u=2),
+                in_=bank[:].rearrange("p a u c -> p a c u"),
+            )
+            return grouped
+
+        def quantise(unit, grouped):
+            nc.vector.quantize_mx(out=unit[1].bitcast(FP8X4), scales=unit[2], in_=grouped[:])
+
+        def passes(m, c):
+            acc = acc_pool.tile([P, CHUNK], F32, name="acc")
+            for g in range(PASSES):
+                cols = slice(P * g, P * g + P)
+                nc.tensor.matmul_mx(
+                    out=acc[:],
+                    lhsT=xq[m][:, cols].bitcast(FP8X4),
+                    lhsT_scale=xs[m][:, cols],
+                    rhs=wq[c][g][:].bitcast(FP8X4),
+                    rhs_scale=ws[c][g][:],
+                    start=(g == 0),
+                    stop=(g == PASSES - 1),
+                )
+            return (m, c, acc)
+
+        def add_bias(group):
+            m, c, acc = group
+            st = st_pool.tile([P, CHUNK], F32, name="st")
+            nc.vector.tensor_tensor(out=st[:], in0=acc[:], in1=bias_bc[:, c * CHUNK:(c + 1) * CHUNK], op=ADD)
+            return (m, c, st)
+
+        def relu_store(summed):
+            m, c, st = summed
+            nc.scalar.activation(out=st[:], in_=st[:], func=RELU)
+            nc.sync.dma_start(out=out_view[m][:, c * CHUNK:(c + 1) * CHUNK], in_=st[:])
+
+        def w_run(c, h):
+            return [w_unit(c, h, g) for g in range(PASSES)]
+
+        def x_run(i):
+            return [x_unit(2 * i + s, gp) for s in range(2) for gp in range(2)]
+
+        cycles = [
+            (w_run(0, 0), []),
+            (w_run(0, 1), []),
+            (x_run(0), []),
+            (x_run(1), [(0, 0), (1, 0)]),
+            (x_run(2), [(2, 0), (3, 0)]),
+            (x_run(3), [(4, 0), (5, 0)]),
+            (w_run(1, 0), [(6, 0)]),
+            (w_run(1, 1), [(7, 0)]),
+            (w_run(2, 0), [(m, 1) for m in range(0, 4)]),
+            (w_run(2, 1), [(m, 1) for m in range(4, 8)]),
+            (w_run(3, 0), [(m, 2) for m in range(0, 4)]),
+            (w_run(3, 1), [(m, 2) for m in range(4, 8)]),
+            ([], [(m, 3) for m in range(0, 8)]),
+        ]
+
+        waiting = None
+        for run, block in cycles:
+            banks = [transposes(unit) for unit in run]
+            tiles = []
+            if run:
+                tiles.append(leave(nc.scalar.copy, banks[0]))
+            if waiting is not None:
+                relu_store(add_bias(waiting))
+                waiting = None
+            if run:
+                tiles.append(leave(nc.scalar.copy, banks[1]))
+                tiles.append(leave(nc.scalar.copy, banks[2]))
+                quantise(run[0], tiles[0])
+                tiles.append(leave(nc.vector.tensor_copy, banks[3]))
+                quantise(run[1], tiles[1])
+                quantise(run[2], tiles[2])
+                quantise(run[3], tiles[3])
+            for m, c in block:
+                if waiting is not None:
+                    relu_store(add_bias(waiting))
+                waiting = passes(m, c)
+        relu_store(add_bias(waiting))

@@ -5,6 +5,7 @@ from concourse.masks import make_identity
 
 F32 = mybir.dt.float32
 BF16 = mybir.dt.bfloat16
+I32 = mybir.dt.int32
 U32 = mybir.dt.uint32
 U8 = mybir.dt.uint8
 FP8X4 = mybir.dt.float8_e4m3fn_x4
@@ -14,19 +15,19 @@ RELU = mybir.ActivationFunctionType.Relu
 P = 128
 B, C, K = 1024, 2048, 2048
 FLOPS = 2 * B * C * K
-PINNED = True
 
 M_TILES = B // P
 CHUNK = 512
 N_CHUNKS = K // CHUNK
 PASSES = C // 512
+WARM_START = 0
+WARM_PER_RUN = [0,0,0]
 
 
 def tile_sparselinearrelu_kernel(tc, x, weight, bias, out):
     nc = tc.nc
     with ExitStack() as ctx:
-        if PINNED:
-            ctx.enter_context(tc.manual_schedule())
+        ctx.enter_context(tc.manual_schedule())
         keep = ctx.enter_context(tc.tile_pool(name="keep", bufs=1))
         grp_pool = ctx.enter_context(tc.tile_pool(name="grp", bufs=8))
         st_pool = ctx.enter_context(tc.tile_pool(name="st", bufs=8))
@@ -37,13 +38,12 @@ def tile_sparselinearrelu_kernel(tc, x, weight, bias, out):
         out_view = out.rearrange("(p t) n -> t p n", t=M_TILES)
         w_view = weight.rearrange("(j p) k -> p j k", p=P)
 
+        ones = keep.tile([P, CHUNK], BF16, name="ones")
+        nc.vector.memset(ones[:], 1.0)
+        brow = keep.tile([P, K], BF16, name="brow")
+        nc.vector.memset(brow[:].bitcast(I32), 0)
         ident = keep.tile([P, P], F32, name="ident")
         make_identity(nc, ident[:])
-        brow = keep.tile([P, K], BF16, name="brow")
-        nc.vector.memset(brow[:], 0.0)
-        nc.sync.dma_start(out=brow[0:1, :], in_=bias.rearrange("(o n) -> o n", o=1))
-        ones = keep.tile([P, P], BF16, name="ones")
-        nc.vector.memset(ones[:], 1.0)
 
         w_sb = {}
         x_sb = {}
@@ -60,6 +60,7 @@ def tile_sparselinearrelu_kernel(tc, x, weight, bias, out):
             x_sb[i] = t
 
         load_w(0, 0)
+        nc.sync.dma_start(out=brow[0:1, :], in_=bias.rearrange("(o n) -> o n", o=1))
         load_w(0, 1)
         for i in range(4):
             load_x(i)
@@ -73,16 +74,18 @@ def tile_sparselinearrelu_kernel(tc, x, weight, bias, out):
               for c in range(N_CHUNKS)]
         ws = [[keep.tile([P, CHUNK], U8, name="ws_%d_%d" % (c, g), align_bytes=64) for g in range(PASSES)]
               for c in range(N_CHUNKS)]
-
         bias_bc = keep.tile([P, K], F32, name="bias_bc")
-        for c in range(N_CHUNKS):
-            cols = slice(c * CHUNK, (c + 1) * CHUNK)
+
+        def warm(n):
+            for i in range(n):
+                wacc = acc_pool.tile([P, CHUNK], F32, name="acc")
+                nc.tensor.matmul(out=wacc[:], lhsT=ones[:, 0:P], rhs=ones[:], start=True, stop=True)
+
+        def bias_matmul(c):
             bacc = acc_pool.tile([P, CHUNK], F32, name="acc")
-            nc.tensor.matmul(out=bacc[:], lhsT=ones[:], rhs=brow[:, cols], start=True, stop=True)
-            if c % 2 == 0:
-                nc.vector.tensor_copy(out=bias_bc[:, cols], in_=bacc[:])
-            else:
-                nc.scalar.copy(out=bias_bc[:, cols], in_=bacc[:])
+            nc.tensor.matmul(out=bacc[:], lhsT=ones[:, 0:P], rhs=brow[:, c * CHUNK:(c + 1) * CHUNK],
+                             start=True, stop=True)
+            return bacc
 
         def w_unit(c, h, g):
             srcs = [w_sb[(c, h)][:, j, :].bitcast(F32)[:, 256 * g:256 * g + 256] for j in range(2)]
@@ -146,24 +149,28 @@ def tile_sparselinearrelu_kernel(tc, x, weight, bias, out):
             return [x_unit(2 * i + s, gp) for s in range(2) for gp in range(2)]
 
         cycles = [
-            (w_run(0, 0), []),
-            (w_run(0, 1), []),
-            (x_run(0), []),
-            (x_run(1), [(0, 0), (1, 0)]),
-            (x_run(2), [(2, 0), (3, 0)]),
-            (x_run(3), [(4, 0), (5, 0)]),
-            (w_run(1, 0), [(6, 0)]),
-            (w_run(1, 1), [(7, 0)]),
-            (w_run(2, 0), [(m, 1) for m in range(0, 4)]),
-            (w_run(2, 1), [(m, 1) for m in range(4, 8)]),
-            (w_run(3, 0), [(m, 2) for m in range(0, 4)]),
-            (w_run(3, 1), [(m, 2) for m in range(4, 8)]),
-            ([], [(m, 3) for m in range(0, 8)]),
+            (w_run(0, 0), [], [0, 1]),
+            (w_run(0, 1), [], [2, 3]),
+            (x_run(0), [], []),
+            (x_run(1), [(0, 0), (1, 0)], []),
+            (x_run(2), [(2, 0), (3, 0)], []),
+            (x_run(3), [(4, 0), (5, 0)], []),
+            (w_run(1, 0), [(6, 0)], []),
+            (w_run(1, 1), [(7, 0)], []),
+            (w_run(2, 0), [(m, 1) for m in range(0, 4)], []),
+            (w_run(2, 1), [(m, 1) for m in range(4, 8)], []),
+            (w_run(3, 0), [(m, 2) for m in range(0, 4)], []),
+            (w_run(3, 1), [(m, 2) for m in range(4, 8)], []),
+            ([], [(m, 3) for m in range(0, 8)], []),
         ]
 
+        warm(WARM_START)
         waiting = None
-        for run, block in cycles:
+        for k, (run, block, bias_chunks) in enumerate(cycles):
             banks = [transposes(unit) for unit in run]
+            baccs = [bias_matmul(c) for c in bias_chunks]
+            if k < len(WARM_PER_RUN):
+                warm(WARM_PER_RUN[k])
             tiles = []
             if run:
                 tiles.append(leave(nc.scalar.copy, banks[0]))
@@ -178,6 +185,9 @@ def tile_sparselinearrelu_kernel(tc, x, weight, bias, out):
                 quantise(run[1], tiles[1])
                 quantise(run[2], tiles[2])
                 quantise(run[3], tiles[3])
+            for i, c in enumerate(bias_chunks):
+                copy = nc.scalar.copy if i % 2 == 0 else nc.vector.tensor_copy
+                copy(out=bias_bc[:, c * CHUNK:(c + 1) * CHUNK], in_=baccs[i][:])
             for m, c in block:
                 if waiting is not None:
                     relu_store(add_bias(waiting))

@@ -20,8 +20,8 @@ M_TILES = B // P
 CHUNK = 512
 N_CHUNKS = K // CHUNK
 PASSES = C // 512
-WARM_START = 0
-WARM_PER_RUN = [0,0,0]
+WARM_START = 8
+WARM_PER_RUN = [3,1,1]
 
 
 def tile_sparselinearrelu_kernel(tc, x, weight, bias, out):
@@ -149,9 +149,9 @@ def tile_sparselinearrelu_kernel(tc, x, weight, bias, out):
             return [x_unit(2 * i + s, gp) for s in range(2) for gp in range(2)]
 
         cycles = [
-            (w_run(0, 0), [], [0, 1]),
-            (w_run(0, 1), [], [2, 3]),
-            (x_run(0), [], []),
+            (w_run(0, 0), [], []),
+            (w_run(0, 1), [], [0, 1]),
+            (x_run(0), [], [2, 3]),
             (x_run(1), [(0, 0), (1, 0)], []),
             (x_run(2), [(2, 0), (3, 0)], []),
             (x_run(3), [(4, 0), (5, 0)], []),

@@ -18,10 +18,11 @@ FLOPS = 2 * B * C * K
 
 M_TILES = B // P
 CHUNK = 512
+HALF = CHUNK // 2
 N_CHUNKS = K // CHUNK
 PASSES = C // 512
 WARM_START = 8
-WARM_PER_RUN = [3,1,1]
+WARM_PER_RUN = 3
 
 
 def tile_sparselinearrelu_kernel(tc, x, weight, bias, out):
@@ -30,7 +31,7 @@ def tile_sparselinearrelu_kernel(tc, x, weight, bias, out):
         ctx.enter_context(tc.manual_schedule())
         keep = ctx.enter_context(tc.tile_pool(name="keep", bufs=1))
         grp_pool = ctx.enter_context(tc.tile_pool(name="grp", bufs=8))
-        st_pool = ctx.enter_context(tc.tile_pool(name="st", bufs=8))
+        st_pool = ctx.enter_context(tc.tile_pool(name="st", bufs=12))
         tp_pool = ctx.enter_context(tc.psum_pool(name="tp", bufs=4))
         acc_pool = ctx.enter_context(tc.psum_pool(name="acc", bufs=4))
 
@@ -61,8 +62,9 @@ def tile_sparselinearrelu_kernel(tc, x, weight, bias, out):
 
         load_w(0, 0)
         nc.sync.dma_start(out=brow[0:1, :], in_=bias.rearrange("(o n) -> o n", o=1))
+        load_x(0)
         load_w(0, 1)
-        for i in range(4):
+        for i in range(1, 4):
             load_x(i)
         for c in range(1, N_CHUNKS):
             load_w(c, 0)
@@ -89,7 +91,7 @@ def tile_sparselinearrelu_kernel(tc, x, weight, bias, out):
 
         def w_unit(c, h, g):
             srcs = [w_sb[(c, h)][:, j, :].bitcast(F32)[:, 256 * g:256 * g + 256] for j in range(2)]
-            cols = slice(256 * h, 256 * h + 256)
+            cols = slice(HALF * h, HALF * h + HALF)
             return srcs, wq[c][g][:, cols], ws[c][g][:, cols]
 
         def x_unit(m, gp):
@@ -116,31 +118,30 @@ def tile_sparselinearrelu_kernel(tc, x, weight, bias, out):
         def quantise(unit, grouped):
             nc.vector.quantize_mx(out=unit[1].bitcast(FP8X4), scales=unit[2], in_=grouped[:])
 
-        def passes(m, c):
-            acc = acc_pool.tile([P, CHUNK], F32, name="acc")
+        def passes(acc, m, c, lo, width):
             for g in range(PASSES):
                 cols = slice(P * g, P * g + P)
                 nc.tensor.matmul_mx(
-                    out=acc[:],
+                    out=acc[:, lo:lo + width],
                     lhsT=xq[m][:, cols].bitcast(FP8X4),
                     lhsT_scale=xs[m][:, cols],
-                    rhs=wq[c][g][:].bitcast(FP8X4),
-                    rhs_scale=ws[c][g][:],
+                    rhs=wq[c][g][:, lo:lo + width].bitcast(FP8X4),
+                    rhs_scale=ws[c][g][:, lo:lo + width],
                     start=(g == 0),
                     stop=(g == PASSES - 1),
                 )
-            return (m, c, acc)
 
-        def add_bias(group):
-            m, c, acc = group
+        def add_bias(done):
+            acc, m, c, lo, width = done
             st = st_pool.tile([P, CHUNK], F32, name="st")
-            nc.vector.tensor_tensor(out=st[:], in0=acc[:], in1=bias_bc[:, c * CHUNK:(c + 1) * CHUNK], op=ADD)
-            return (m, c, st)
+            nc.vector.tensor_tensor(out=st[:, 0:width], in0=acc[:, lo:lo + width],
+                                    in1=bias_bc[:, c * CHUNK + lo:c * CHUNK + lo + width], op=ADD)
+            return st, m, c, lo, width
 
         def relu_store(summed):
-            m, c, st = summed
-            nc.scalar.activation(out=st[:], in_=st[:], func=RELU)
-            nc.sync.dma_start(out=out_view[m][:, c * CHUNK:(c + 1) * CHUNK], in_=st[:])
+            st, m, c, lo, width = summed
+            nc.scalar.activation(out=st[:, 0:width], in_=st[:, 0:width], func=RELU)
+            nc.sync.dma_start(out=out_view[m][:, c * CHUNK + lo:c * CHUNK + lo + width], in_=st[:, 0:width])
 
         def w_run(c, h):
             return [w_unit(c, h, g) for g in range(PASSES)]
@@ -148,48 +149,64 @@ def tile_sparselinearrelu_kernel(tc, x, weight, bias, out):
         def x_run(i):
             return [x_unit(2 * i + s, gp) for s in range(2) for gp in range(2)]
 
+        def whole(ms, c):
+            return [(m, c, 0, CHUNK, "whole") for m in ms]
+
         cycles = [
-            (w_run(0, 0), [], []),
-            (w_run(0, 1), [], [0, 1]),
-            (x_run(0), [], [2, 3]),
-            (x_run(1), [(0, 0), (1, 0)], []),
-            (x_run(2), [(2, 0), (3, 0)], []),
-            (x_run(3), [(4, 0), (5, 0)], []),
-            (w_run(1, 0), [(6, 0)], []),
-            (w_run(1, 1), [(7, 0)], []),
-            (w_run(2, 0), [(m, 1) for m in range(0, 4)], []),
-            (w_run(2, 1), [(m, 1) for m in range(4, 8)], []),
-            (w_run(3, 0), [(m, 2) for m in range(0, 4)], []),
-            (w_run(3, 1), [(m, 2) for m in range(4, 8)], []),
-            ([], [(m, 3) for m in range(0, 8)], []),
+            (w_run(0, 0), "warm", []),
+            (x_run(0), "bias", []),
+            (w_run(0, 1), "", [(0, 0, 0, HALF, "first"), (1, 0, 0, HALF, "first")]),
+            (x_run(1), "", [(0, 0, HALF, HALF, "second"), (1, 0, HALF, HALF, "second")]),
+            (x_run(2), "", whole([2, 3], 0)),
+            (x_run(3), "", whole([4, 5], 0)),
+            (w_run(1, 0), "", whole([6], 0)),
+            (w_run(1, 1), "", whole([7], 0)),
+            (w_run(2, 0), "", whole(range(0, 4), 1)),
+            (w_run(2, 1), "", whole(range(4, 8), 1)),
+            (w_run(3, 0), "", whole(range(0, 4), 2)),
+            (w_run(3, 1), "", whole(range(4, 8), 2)),
+            ([], "", whole(range(0, 7), 3) + [(7, 3, 0, HALF, "part"), (7, 3, HALF, HALF, "part")]),
         ]
 
         warm(WARM_START)
         waiting = None
-        for k, (run, block, bias_chunks) in enumerate(cycles):
+        held = {}
+        for run, plain, block in cycles:
             banks = [transposes(unit) for unit in run]
-            baccs = [bias_matmul(c) for c in bias_chunks]
-            if k < len(WARM_PER_RUN):
-                warm(WARM_PER_RUN[k])
-            tiles = []
-            if run:
-                tiles.append(leave(nc.scalar.copy, banks[0]))
+            baccs = []
+            if plain == "warm":
+                warm(WARM_PER_RUN)
+            if plain == "bias":
+                baccs = [bias_matmul(c) for c in range(N_CHUNKS)]
+            summed = None
             if waiting is not None:
-                relu_store(add_bias(waiting))
+                summed = add_bias(waiting)
                 waiting = None
+            tiles = [leave(nc.scalar.copy, bank) for bank in banks[0:3]]
+            if summed is not None:
+                relu_store(summed)
             if run:
-                tiles.append(leave(nc.scalar.copy, banks[1]))
-                tiles.append(leave(nc.scalar.copy, banks[2]))
                 quantise(run[0], tiles[0])
                 tiles.append(leave(nc.vector.tensor_copy, banks[3]))
                 quantise(run[1], tiles[1])
                 quantise(run[2], tiles[2])
                 quantise(run[3], tiles[3])
-            for i, c in enumerate(bias_chunks):
-                copy = nc.scalar.copy if i % 2 == 0 else nc.vector.tensor_copy
-                copy(out=bias_bc[:, c * CHUNK:(c + 1) * CHUNK], in_=baccs[i][:])
-            for m, c in block:
+            for c, bacc in enumerate(baccs):
+                copy = nc.scalar.copy if c % 2 == 0 else nc.vector.tensor_copy
+                copy(out=bias_bc[:, c * CHUNK:(c + 1) * CHUNK], in_=bacc[:])
+            for m, c, lo, width, kind in block:
                 if waiting is not None:
                     relu_store(add_bias(waiting))
-                waiting = passes(m, c)
+                    waiting = None
+                if kind == "second":
+                    acc = held[(m, c)]
+                else:
+                    acc = acc_pool.tile([P, CHUNK], F32, name="acc")
+                passes(acc, m, c, lo, width)
+                if kind == "first":
+                    held[(m, c)] = acc
+                elif kind == "second":
+                    waiting = (acc, m, c, 0, CHUNK)
+                else:
+                    waiting = (acc, m, c, lo, width)
         relu_store(add_bias(waiting))

@@ -161,10 +161,8 @@ def tile_sparselinearrelu_kernel(tc, x, weight, bias, out):
             (x_run(3), "", whole([4, 5], 0)),
             (w_run(1, 0), "", whole([6], 0)),
             (w_run(1, 1), "", whole([7], 0)),
-            (w_run(2, 0), "", whole(range(0, 4), 1)),
-            (w_run(2, 1), "", whole(range(4, 8), 1)),
-            (w_run(3, 0), "", whole(range(0, 4), 2)),
-            (w_run(3, 1), "", whole(range(4, 8), 2)),
+            (w_run(2, 0) + w_run(2, 1), "", whole(range(0, 8), 1)),
+            (w_run(3, 0) + w_run(3, 1), "", whole(range(0, 8), 2)),
             ([], "", whole(range(0, 7), 3) + [(7, 3, 0, HALF, "part"), (7, 3, HALF, HALF, "part")]),
         ]
 
@@ -172,7 +170,8 @@ def tile_sparselinearrelu_kernel(tc, x, weight, bias, out):
         waiting = None
         held = {}
         for run, plain, block in cycles:
-            banks = [transposes(unit) for unit in run]
+            long_run = len(run) == 8
+            banks = [] if long_run else [transposes(unit) for unit in run]
             baccs = []
             if plain == "warm":
                 warm(WARM_PER_RUN)
@@ -183,9 +182,15 @@ def tile_sparselinearrelu_kernel(tc, x, weight, bias, out):
                 summed = add_bias(waiting)
                 waiting = None
             tiles = [leave(nc.scalar.copy, bank) for bank in banks[0:3]]
+            if long_run:
+                for i, unit in enumerate(run):
+                    tiles.append(leave(nc.vector.tensor_copy if i % 3 == 2 else nc.scalar.copy, transposes(unit)))
             if summed is not None:
                 relu_store(summed)
-            if run:
+            if long_run:
+                for unit, grouped in zip(run, tiles):
+                    quantise(unit, grouped)
+            elif run:
                 quantise(run[0], tiles[0])
                 tiles.append(leave(nc.vector.tensor_copy, banks[3]))
                 quantise(run[1], tiles[1])

@@ -31,7 +31,7 @@ def tile_sparselinearrelu_kernel(tc, x, weight, bias, out):
         ctx.enter_context(tc.manual_schedule())
         keep = ctx.enter_context(tc.tile_pool(name="keep", bufs=1))
         grp_pool = ctx.enter_context(tc.tile_pool(name="grp", bufs=8))
-        st_pool = ctx.enter_context(tc.tile_pool(name="st", bufs=12))
+        st_pool = ctx.enter_context(tc.tile_pool(name="st", bufs=16))
         tp_pool = ctx.enter_context(tc.psum_pool(name="tp", bufs=4))
         acc_pool = ctx.enter_context(tc.psum_pool(name="acc", bufs=4))
 
@@ -161,36 +161,32 @@ def tile_sparselinearrelu_kernel(tc, x, weight, bias, out):
             (x_run(3), "", whole([4, 5], 0)),
             (w_run(1, 0), "", whole([6], 0)),
             (w_run(1, 1), "", whole([7], 0)),
-            (w_run(2, 0) + w_run(2, 1), "", whole(range(0, 8), 1)),
-            (w_run(3, 0) + w_run(3, 1), "", whole(range(0, 8), 2)),
+            (w_run(2, 0), "", whole(range(0, 4), 1)),
+            (w_run(2, 1), "", whole(range(4, 8), 1)),
+            (w_run(3, 0), "", whole(range(0, 4), 2)),
+            (w_run(3, 1), "", whole(range(4, 8), 2)),
             ([], "", whole(range(0, 7), 3) + [(7, 3, 0, HALF, "part"), (7, 3, HALF, HALF, "part")]),
         ]
 
         warm(WARM_START)
         waiting = None
+        pending = []
         held = {}
         for run, plain, block in cycles:
-            long_run = len(run) == 8
-            banks = [] if long_run else [transposes(unit) for unit in run]
+            banks = [transposes(unit) for unit in run]
             baccs = []
             if plain == "warm":
                 warm(WARM_PER_RUN)
             if plain == "bias":
                 baccs = [bias_matmul(c) for c in range(N_CHUNKS)]
-            summed = None
             if waiting is not None:
-                summed = add_bias(waiting)
+                pending.append(add_bias(waiting))
                 waiting = None
             tiles = [leave(nc.scalar.copy, bank) for bank in banks[0:3]]
-            if long_run:
-                for i, unit in enumerate(run):
-                    tiles.append(leave(nc.vector.tensor_copy if i % 3 == 2 else nc.scalar.copy, transposes(unit)))
-            if summed is not None:
+            for summed in pending:
                 relu_store(summed)
-            if long_run:
-                for unit, grouped in zip(run, tiles):
-                    quantise(unit, grouped)
-            elif run:
+            pending = []
+            if run:
                 quantise(run[0], tiles[0])
                 tiles.append(leave(nc.vector.tensor_copy, banks[3]))
                 quantise(run[1], tiles[1])
@@ -201,8 +197,12 @@ def tile_sparselinearrelu_kernel(tc, x, weight, bias, out):
                 copy(out=bias_bc[:, c * CHUNK:(c + 1) * CHUNK], in_=bacc[:])
             for m, c, lo, width, kind in block:
                 if waiting is not None:
-                    relu_store(add_bias(waiting))
+                    pending.append(add_bias(waiting))
                     waiting = None
+                if not run:
+                    for summed in pending:
+                        relu_store(summed)
+                    pending = []
                 if kind == "second":
                     acc = held[(m, c)]
                 else:

from contextlib import ExitStack

import concourse.mybir as mybir
from concourse.masks import make_identity

F32 = mybir.dt.float32
BF16 = mybir.dt.bfloat16
I32 = mybir.dt.int32
U32 = mybir.dt.uint32
U8 = mybir.dt.uint8
FP8X4 = mybir.dt.float8_e4m3fn_x4
ADD = mybir.AluOpType.add
RELU = mybir.ActivationFunctionType.Relu

P = 128
B, C, K = 1024, 2048, 2048
FLOPS = 2 * B * C * K

M_TILES = B // P
CHUNK = 512
HALF = CHUNK // 2
N_CHUNKS = K // CHUNK
PASSES = C // 512
WARM_START = 8
WARM_PER_RUN = 3


def tile_sparselinearrelu_kernel(tc, x, weight, bias, out):
    nc = tc.nc
    with ExitStack() as ctx:
        ctx.enter_context(tc.manual_schedule())
        keep = ctx.enter_context(tc.tile_pool(name="keep", bufs=1))
        grp_pool = ctx.enter_context(tc.tile_pool(name="grp", bufs=8))
        st_pool = ctx.enter_context(tc.tile_pool(name="st", bufs=16))
        tp_pool = ctx.enter_context(tc.psum_pool(name="tp", bufs=4))
        acc_pool = ctx.enter_context(tc.psum_pool(name="acc", bufs=4))

        x_view = x.rearrange("(p t) k -> p t k", t=M_TILES)
        out_view = out.rearrange("(p t) n -> t p n", t=M_TILES)
        w_view = weight.rearrange("(j p) k -> p j k", p=P)

        ones = keep.tile([P, CHUNK], BF16, name="ones")
        nc.vector.memset(ones[:], 1.0)
        brow = keep.tile([P, K], BF16, name="brow")
        nc.vector.memset(brow[:].bitcast(I32), 0)
        ident = keep.tile([P, P], F32, name="ident")
        make_identity(nc, ident[:])

        w_sb = {}
        x_sb = {}

        def load_w(c, h):
            t = keep.tile([P, 2, C], BF16, name="w_sb_%d_%d" % (c, h))
            j0 = 4 * c + 2 * h
            nc.sync.dma_start(out=t[:], in_=w_view[:, j0:j0 + 2, :])
            w_sb[(c, h)] = t

        def load_x(i):
            t = keep.tile([P, 2, C], BF16, name="x_sb_%d" % i)
            nc.sync.dma_start(out=t[:], in_=x_view[:, 2 * i:2 * i + 2, :])
            x_sb[i] = t

        load_w(0, 0)
        nc.sync.dma_start(out=brow[0:1, :], in_=bias.rearrange("(o n) -> o n", o=1))
        load_x(0)
        load_w(0, 1)
        for i in range(1, 4):
            load_x(i)
        for c in range(1, N_CHUNKS):
            load_w(c, 0)
            load_w(c, 1)

        xq = [keep.tile([P, PASSES * P], U32, name="xq_%d" % m, align_bytes=64) for m in range(M_TILES)]
        xs = [keep.tile([P, PASSES * P], U8, name="xs_%d" % m, align_bytes=64) for m in range(M_TILES)]
        wq = [[keep.tile([P, CHUNK], U32, name="wq_%d_%d" % (c, g), align_bytes=64) for g in range(PASSES)]
              for c in range(N_CHUNKS)]
        ws = [[keep.tile([P, CHUNK], U8, name="ws_%d_%d" % (c, g), align_bytes=64) for g in range(PASSES)]
              for c in range(N_CHUNKS)]
        bias_bc = keep.tile([P, K], F32, name="bias_bc")

        def warm(n):
            for i in range(n):
                wacc = acc_pool.tile([P, CHUNK], F32, name="acc")
                nc.tensor.matmul(out=wacc[:], lhsT=ones[:, 0:P], rhs=ones[:], start=True, stop=True)

        def bias_matmul(c):
            bacc = acc_pool.tile([P, CHUNK], F32, name="acc")
            nc.tensor.matmul(out=bacc[:], lhsT=ones[:, 0:P], rhs=brow[:, c * CHUNK:(c + 1) * CHUNK],
                             start=True, stop=True)
            return bacc

        def w_unit(c, h, g):
            srcs = [w_sb[(c, h)][:, j, :].bitcast(F32)[:, 256 * g:256 * g + 256] for j in range(2)]
            cols = slice(HALF * h, HALF * h + HALF)
            return srcs, wq[c][g][:, cols], ws[c][g][:, cols]

        def x_unit(m, gp):
            row = x_sb[m // 2][:, m % 2, :].bitcast(F32)
            srcs = [row[:, 256 * (2 * gp + a):256 * (2 * gp + a) + 256] for a in range(2)]
            cols = slice(256 * gp, 256 * gp + 256)
            return srcs, xq[m][:, cols], xs[m][:, cols]

        def transposes(unit):
            bank = tp_pool.tile([P, 2, 2, P], F32, name="bank")
            for a in range(2):
                for u in range(2):
                    nc.tensor.transpose(bank[:, a, u, :], unit[0][a][:, P * u:P * u + P], ident[:])
            return bank

        def leave(engine_copy, bank):
            grouped = grp_pool.tile([P, 1024], BF16, name="grouped", align_bytes=64)
            engine_copy(
                out=grouped[:].bitcast(F32).rearrange("p (a c u) -> p a c u", a=2, u=2),
                in_=bank[:].rearrange("p a u c -> p a c u"),
            )
            return grouped

        def quantise(unit, grouped):
            nc.vector.quantize_mx(out=unit[1].bitcast(FP8X4), scales=unit[2], in_=grouped[:])

        def passes(acc, m, c, lo, width):
            for g in range(PASSES):
                cols = slice(P * g, P * g + P)
                nc.tensor.matmul_mx(
                    out=acc[:, lo:lo + width],
                    lhsT=xq[m][:, cols].bitcast(FP8X4),
                    lhsT_scale=xs[m][:, cols],
                    rhs=wq[c][g][:, lo:lo + width].bitcast(FP8X4),
                    rhs_scale=ws[c][g][:, lo:lo + width],
                    start=(g == 0),
                    stop=(g == PASSES - 1),
                )

        def add_bias(done):
            acc, m, c, lo, width = done
            st = st_pool.tile([P, CHUNK], F32, name="st")
            nc.vector.tensor_tensor(out=st[:, 0:width], in0=acc[:, lo:lo + width],
                                    in1=bias_bc[:, c * CHUNK + lo:c * CHUNK + lo + width], op=ADD)
            return st, m, c, lo, width

        def relu_store(summed):
            st, m, c, lo, width = summed
            nc.scalar.activation(out=st[:, 0:width], in_=st[:, 0:width], func=RELU)
            nc.sync.dma_start(out=out_view[m][:, c * CHUNK + lo:c * CHUNK + lo + width], in_=st[:, 0:width])

        def w_run(c, h):
            return [w_unit(c, h, g) for g in range(PASSES)]

        def x_run(i):
            return [x_unit(2 * i + s, gp) for s in range(2) for gp in range(2)]

        def whole(ms, c):
            return [(m, c, 0, CHUNK, "whole") for m in ms]

        cycles = [
            (w_run(0, 0), "warm", []),
            (x_run(0), "bias", []),
            (w_run(0, 1), "", [(0, 0, 0, HALF, "first"), (1, 0, 0, HALF, "first")]),
            (x_run(1), "", [(0, 0, HALF, HALF, "second"), (1, 0, HALF, HALF, "second")]),
            (x_run(2), "", whole([2, 3], 0)),
            (x_run(3), "", whole([4, 5], 0)),
            (w_run(1, 0), "", whole([6], 0)),
            (w_run(1, 1), "", whole([7], 0)),
            (w_run(2, 0), "", whole(range(0, 4), 1)),
            (w_run(2, 1), "", whole(range(4, 8), 1)),
            (w_run(3, 0), "", whole(range(0, 4), 2)),
            (w_run(3, 1), "", whole(range(4, 8), 2)),
            ([], "", whole(range(0, 7), 3) + [(7, 3, 0, HALF, "part"), (7, 3, HALF, HALF, "part")]),
        ]

        warm(WARM_START)
        waiting = None
        pending = []
        held = {}
        for run, plain, block in cycles:
            banks = [transposes(unit) for unit in run]
            baccs = []
            if plain == "warm":
                warm(WARM_PER_RUN)
            if plain == "bias":
                baccs = [bias_matmul(c) for c in range(N_CHUNKS)]
            if waiting is not None:
                pending.append(add_bias(waiting))
                waiting = None
            tiles = [leave(nc.scalar.copy, bank) for bank in banks[0:3]]
            for summed in pending:
                relu_store(summed)
            pending = []
            if run:
                quantise(run[0], tiles[0])
                tiles.append(leave(nc.vector.tensor_copy, banks[3]))
                quantise(run[1], tiles[1])
                quantise(run[2], tiles[2])
                quantise(run[3], tiles[3])
            for c, bacc in enumerate(baccs):
                copy = nc.scalar.copy if c % 2 == 0 else nc.vector.tensor_copy
                copy(out=bias_bc[:, c * CHUNK:(c + 1) * CHUNK], in_=bacc[:])
            for m, c, lo, width, kind in block:
                if waiting is not None:
                    pending.append(add_bias(waiting))
                    waiting = None
                if not run:
                    for summed in pending:
                        relu_store(summed)
                    pending = []
                if kind == "second":
                    acc = held[(m, c)]
                else:
                    acc = acc_pool.tile([P, CHUNK], F32, name="acc")
                passes(acc, m, c, lo, width)
                if kind == "first":
                    held[(m, c)] = acc
                elif kind == "second":
                    waiting = (acc, m, c, 0, CHUNK)
                else:
                    waiting = (acc, m, c, lo, width)
        relu_store(add_bias(waiting))
